import numpy as np
import ml_dtypes


def mxq(x, axis, fmt="e4m3"):
    dtype, down = {"e4m3": (ml_dtypes.float8_e4m3fn, 7), "e5m2": (ml_dtypes.float8_e5m2, 14)}[fmt]
    v = np.moveaxis(np.asarray(x, np.float32).astype(ml_dtypes.bfloat16).astype(np.float64), axis, -1)
    blocks = v.reshape(v.shape[:-1] + (-1, 32))
    amax = np.abs(blocks).max(-1, keepdims=True)
    byte = np.maximum(np.where(amax > 0, np.frexp(amax)[1] - 1 + 127, 0) - down, 1)
    scale = np.exp2(byte - 127.0)
    codes = (blocks / scale).astype(np.float32).astype(dtype).astype(np.float64)
    return np.moveaxis((codes * scale).reshape(v.shape), -1, axis)


WIDE = False


def mx_kscale(k):
    if not WIDE:
        return np.ones(k)
    levels = np.array([10, -10, 5, -5, 0])
    if k % 512:
        return np.exp2(np.random.permutation(np.resize(levels, k // 32))).repeat(32)
    a = np.empty((k // 512, 16))
    for p in range(k // 512):
        a[p, :8] = np.random.permutation(np.resize(levels, 8))
        for g in range(8):
            far = levels[np.abs(levels - a[p, g]) >= 10]
            a[p, g + 8] = far[np.random.randint(len(far))]
    return np.exp2(a.ravel()).repeat(32)


BF16 = ml_dtypes.bfloat16


def bf(x):
    return np.asarray(x, np.float32).astype(BF16)


def f64(x):
    return np.asarray(x).astype(np.float64)


B, S, DIM, QL, KVL, H, DN, DR, DV, P0 = 4, 2048, 512, 512, 512, 4, 16, 16, 128, 37
EPS = 1e-6
HALF = DR // 2


def rms_norm(v, w):
    return v / np.sqrt(np.mean(v * v, axis=-1, keepdims=True) + EPS) * w


def rope(v, start):
    theta = 10000.0 ** (-np.arange(HALF) / HALF)
    pos = np.arange(v.shape[-2]) + start
    ang = pos[:, None] * theta[None, :]
    ang2 = np.concatenate([ang, ang], axis=-1)
    v1, v2 = v[..., :HALF], v[..., HALF:]
    rot = np.concatenate([-v2, v1], axis=-1)
    return v * np.cos(ang2) + rot * np.sin(ang2)


def setup_inputs():
    s, t = mx_kscale(DIM), mx_kscale(QL)
    return {"x": bf(np.random.standard_normal((B, S, DIM)) * s),
            "wq_a": bf(np.random.standard_normal((DIM, QL)) / np.sqrt(DIM) / s[:, None]),
            "q_norm_w": bf((1.0 + 0.1 * np.random.standard_normal(QL)) * t),
            "wq_b": bf(np.random.standard_normal((QL, H * (DN + DR))) / np.sqrt(QL) / t[:, None])}


def reference(x, wq_a, q_norm_w, wq_b):
    c = mxq(f64(x), 2, "e4m3") @ mxq(f64(wq_a), 0, "e4m3")
    cn = rms_norm(c, f64(q_norm_w))
    q = (mxq(cn, 2, "e4m3") @ mxq(f64(wq_b), 0, "e4m3")).reshape(B, S, H, DN + DR)
    q_nope, q_rope = q[..., :DN], q[..., DN:]
    q_rope = rope(q_rope.reshape(B, H, S, DR), P0).reshape(B, S, H, DR)
    return np.concatenate([q_nope, q_rope], axis=-1)

@@ -1,0 +1,277 @@
+import math
+from contextlib import ExitStack
+
+import concourse.mybir as mybir
+from concourse.masks import make_identity
+
+F32 = mybir.dt.float32
+BF16 = mybir.dt.bfloat16
+U32 = mybir.dt.uint32
+U8 = mybir.dt.uint8
+FP8X4 = mybir.dt.float8_e4m3fn_x4
+ALU = mybir.AluOpType
+ACT = mybir.ActivationFunctionType
+
+P = 128
+PACK = 4
+K = P * PACK
+TOKENS = 4 * 2048
+QL = 512
+OUT = 128
+HEAD = 32
+ROT = 16
+HALF = ROT // 2
+START = 37
+EPS = 1e-6
+GROUP = 4
+PAIR = 2
+N_GROUPS = TOKENS // (GROUP * P)
+PAIRS_IN_GROUP = GROUP // PAIR
+N_PAIRS = N_GROUPS * PAIRS_IN_GROUP
+VECS = GROUP * OUT // HEAD
+
+TWO_PI = 2.0 * math.pi
+TWO_PI_HIGH = 6.28125
+TWO_PI_LOW = TWO_PI - TWO_PI_HIGH
+ROUND_MAGIC = 1.5 * 2.0**23
+
+FLOPS = 2 * TOKENS * K * (QL + OUT)
+
+
+def load_weight(pool, queue, w, cols, label):
+    raw = pool.tile([P, PACK * cols], BF16, name="%s_raw" % label)
+    queue.dma_start(
+        out=raw[:],
+        in_=w.rearrange("(p t) c -> p (t c)", p=P),
+    )
+    return raw
+
+
+def regroup_weight(copy, raw, grouped, cols):
+    copy(
+        out=grouped[:].rearrange("p (c t) -> p c t", t=PACK)[:, cols, :],
+        in_=raw[:].rearrange("p (t c) -> p c t", t=PACK)[:, cols, :],
+    )
+
+
+def quantise_weight(nc, pool, grouped, cols, label):
+    codes = pool.tile([P, cols], U32, name="%s_codes" % label, align_bytes=64)
+    scales = pool.tile([P, cols], U8, name="%s_scales" % label, align_bytes=64)
+    nc.vector.quantize_mx(out=codes[:].bitcast(FP8X4), scales=scales[:], in_=grouped[:])
+    return codes, scales
+
+
+def rope_angles(nc, pool):
+    pos = pool.tile([P, VECS], F32)
+    nc.gpsimd.iota(
+        pos[:], pattern=[[1, VECS]], base=START, channel_multiplier=VECS, allow_small_or_imprecise_dtypes=True
+    )
+    angle = pool.tile([P, 2, VECS, HALF], F32)
+    for j in range(HALF):
+        theta = 10000.0 ** (-j / HALF)
+        nc.vector.tensor_scalar(out=angle[:, 0, :, j], in0=pos[:], scalar1=theta, scalar2=None, op0=ALU.mult)
+        nc.vector.tensor_scalar(
+            out=angle[:, 1, :, j], in0=pos[:], scalar1=theta, scalar2=0.5 * math.pi, op0=ALU.mult, op1=ALU.add
+        )
+    return angle
+
+
+def take_off_turns(nc, angle, turns):
+    flat = angle[:].rearrange("p s v j -> p (s v j)")
+    nc.vector.tensor_scalar(
+        out=turns[:], in0=flat, scalar1=1.0 / TWO_PI, scalar2=ROUND_MAGIC, op0=ALU.mult, op1=ALU.add
+    )
+    nc.vector.tensor_scalar(out=turns[:], in0=turns[:], scalar1=ROUND_MAGIC, scalar2=None, op0=ALU.subtract)
+    for part in (TWO_PI_HIGH, TWO_PI_LOW):
+        nc.vector.scalar_tensor_tensor(out=flat, in0=turns[:], scalar=-part, in1=flat, op0=ALU.mult, op1=ALU.add)
+
+
+def rope_tables(nc, pool, angle):
+    cos32 = pool.tile([P, VECS, HEAD], F32)
+    nc.vector.memset(cos32[:], 1.0)
+    nc.scalar.activation(out=cos32[:, :, ROT : ROT + HALF], in_=angle[:, 1], func=ACT.Sin)
+    nc.scalar.activation(out=cos32[:, :, ROT + HALF : HEAD], in_=angle[:, 1], func=ACT.Sin)
+    sin16 = pool.tile([P, VECS, ROT], F32)
+    nc.scalar.activation(out=sin16[:, :, 0:HALF], in_=angle[:, 0], func=ACT.Sin, scale=-1.0)
+    nc.scalar.activation(out=sin16[:, :, HALF:ROT], in_=angle[:, 0], func=ACT.Sin)
+    return cos32, sin16
+
+
+def tile_mla_pa_t_kernel(tc, x, wq_a, q_norm_w, wq_b, out):
+    nc = tc.nc
+    x_groups = x.rearrange("b (c p a) k -> (b c) p (a k)", p=P, a=GROUP)
+    out_groups = out.rearrange("b (c p a) h d -> (b c) p (a h d)", p=P, a=GROUP)
+
+    with ExitStack() as ctx:
+        const = ctx.enter_context(tc.tile_pool(name="const", bufs=1))
+        x_pool = ctx.enter_context(tc.tile_pool(name="x_pool", bufs=N_PAIRS))
+        work = ctx.enter_context(tc.tile_pool(name="work", bufs=3))
+        psum_t = ctx.enter_context(tc.psum_pool(name="psum_t", bufs=1))
+        psum_c = ctx.enter_context(tc.psum_pool(name="psum_c", bufs=4))
+        psum_q = ctx.enter_context(tc.psum_pool(name="psum_q", bufs=2))
+        ctx.enter_context(tc.manual_schedule())
+
+        wa_raw = load_weight(const, nc.sync, wq_a, QL, "wa")
+        x_tiles = []
+        for i in range(N_PAIRS):
+            g, h = divmod(i, PAIRS_IN_GROUP)
+            x_sb = x_pool.tile([P, PAIR * K], BF16)
+            nc.sync.dma_start(out=x_sb[:], in_=x_groups[g][:, h * PAIR * K : (h + 1) * PAIR * K])
+            x_tiles.append(x_sb)
+        wb_raw = load_weight(const, nc.scalar, wq_b, OUT, "wb")
+        gain = const.tile([P, QL], BF16)
+        nc.scalar.dma_start(out=gain[:], in_=q_norm_w.partition_broadcast(P))
+
+        warm = const.tile([P, 1], F32)
+        nc.vector.memset(warm[:], 0.0)
+        nc.scalar.activation(out=warm[:], in_=warm[:], func=ACT.Sin)
+
+        ident = const.tile([P, P], F32)
+        make_identity(nc, ident[:])
+        eps = const.tile([P, 1], F32)
+        nc.vector.memset(eps[:], EPS)
+        angle = rope_angles(nc, const)
+        turns = const.tile([P, 2 * VECS * HALF], F32)
+        take_off_turns(nc, angle, turns)
+        wa_grouped = const.tile([P, QL * PACK], BF16, align_bytes=64)
+        wb_grouped = const.tile([P, OUT * PACK], BF16, align_bytes=64)
+        regroup_weight(nc.scalar.copy, wa_raw, wa_grouped, slice(QL // 2, QL))
+        regroup_weight(nc.gpsimd.tensor_copy, wb_raw, wb_grouped, slice(0, OUT))
+        regroup_weight(nc.vector.tensor_copy, wa_raw, wa_grouped, slice(0, QL // 2))
+        wa_codes, wa_scales = quantise_weight(nc, const, wa_grouped, QL, "wa")
+        take_off_turns(nc, angle, turns)
+        wb_codes, wb_scales = quantise_weight(nc, const, wb_grouped, OUT, "wb")
+
+        def transpose_pair(words, label):
+            bank = psum_t.tile([P, PAIR, 2, P], F32, name="%s_bank" % label)
+            for a in range(PAIR):
+                for u in range(2):
+                    nc.tensor.transpose(
+                        bank[:, a, u, :], words[:, 2 * a * P + u : 2 * (a + 1) * P : 2], ident[:]
+                    )
+            return bank
+
+        def regroup_pair(bank, label):
+            grouped = work.tile([P, PAIR * K], BF16, name="%s_grouped" % label, align_bytes=64)
+            nc.scalar.copy(
+                out=grouped[:].bitcast(F32).rearrange("p (a t u) -> p a t u", a=PAIR, u=2),
+                in_=bank[:].rearrange("p a u t -> p a t u"),
+            )
+            return grouped
+
+        def quantise_pair(grouped, label):
+            codes = work.tile([P, PAIR * P], U32, name="%s_codes" % label, align_bytes=64)
+            scales = work.tile([P, PAIR * P], U8, name="%s_scales" % label, align_bytes=64)
+            nc.vector.quantize_mx(out=codes[:].bitcast(FP8X4), scales=scales[:], in_=grouped[:])
+            return codes, scales
+
+        def multiply(acc, operand, a, w_codes, w_scales):
+            codes, scales = operand
+            tokens = slice(a * P, (a + 1) * P)
+            nc.tensor.matmul_mx(
+                out=acc,
+                lhsT=codes[:, tokens].bitcast(FP8X4),
+                lhsT_scale=scales[:, tokens],
+                rhs=w_codes[:].bitcast(FP8X4),
+                rhs_scale=w_scales[:],
+                start=True,
+                stop=True,
+            )
+
+        def first_matmul(operand):
+            banks = []
+            for a in range(PAIR):
+                c_bank = psum_c.tile([P, QL], F32)
+                multiply(c_bank[:], operand, a, wa_codes, wa_scales)
+                banks.append(c_bank)
+            return banks
+
+        def inverse_rms(banks):
+            sum_sq = work.tile([P, PAIR], F32)
+            for a in range(PAIR):
+                squares = work.tile([P, QL], BF16)
+                nc.scalar.activation(
+                    out=squares[:], in_=banks[a][:], func=ACT.Square, accum_out=sum_sq[:, a : a + 1]
+                )
+            inv_rms = work.tile([P, PAIR], F32)
+            nc.scalar.activation(
+                out=inv_rms[:], in_=sum_sq[:], func=ACT.Abs_reciprocal_sqrt, scale=1.0 / QL, bias=eps[:]
+            )
+            return inv_rms
+
+        def normalise(banks, inv_rms):
+            cn = work.tile([P, PAIR * QL], BF16)
+            for a in range(PAIR):
+                nc.vector.scalar_tensor_tensor(
+                    out=cn[:, a * QL : (a + 1) * QL],
+                    in0=banks[a][:],
+                    scalar=inv_rms[:, a : a + 1],
+                    in1=gain[:],
+                    op0=ALU.mult,
+                    op1=ALU.mult,
+                )
+            return cn
+
+        def rope_straight(q_bank):
+            result = work.tile([P, VECS, HEAD], F32)
+            q = q_bank[:].rearrange("p a (h d) -> p (a h) d", d=HEAD)
+            nc.vector.tensor_tensor(out=result[:], in0=q, in1=cos32[:], op=ALU.mult)
+            return result
+
+        def rope_crossed(q_bank, result, g):
+            q = q_bank[:].rearrange("p a (h d) -> p (a h) d", d=HEAD)
+            crossed = work.tile([P, VECS, ROT], F32)
+            nc.vector.tensor_tensor(
+                out=crossed[:, :, 0:HALF], in0=q[:, :, ROT + HALF : HEAD], in1=sin16[:, :, 0:HALF], op=ALU.mult
+            )
+            nc.vector.tensor_tensor(
+                out=crossed[:, :, HALF:ROT], in0=q[:, :, ROT : ROT + HALF], in1=sin16[:, :, HALF:ROT], op=ALU.mult
+            )
+            nc.vector.tensor_tensor(
+                out=result[:, :, ROT:HEAD], in0=result[:, :, ROT:HEAD], in1=crossed[:], op=ALU.add
+            )
+            nc.sync.dma_start(out=out_groups[g], in_=result[:].rearrange("p v d -> p (v d)"))
+
+        def live(i):
+            return 0 <= i < N_PAIRS
+
+        x_bank_of, x_grouped_of, x_mx_of, c_banks_of, inv_rms_of = {}, {}, {}, {}, {}
+        cn_of, cn_bank_of, cn_grouped_of, cn_mx_of = {}, {}, {}, {}
+        q_bank_of, result_of = {}, {}
+        def one_round(i):
+            if live(i + 2):
+                x_bank_of[i + 2] = transpose_pair(x_tiles[i + 2][:].bitcast(F32), "x")
+            if live(i - 1):
+                cn_bank_of[i - 1] = transpose_pair(cn_of[i - 1][:].bitcast(F32), "cn")
+            if live(i + 1):
+                x_mx_of[i + 1] = quantise_pair(x_grouped_of[i + 1], "x")
+            if live(i - 2):
+                cn_mx_of[i - 2] = quantise_pair(cn_grouped_of[i - 2], "cn")
+            if live(i + 1):
+                c_banks_of[i + 1] = first_matmul(x_mx_of[i + 1])
+            if live(i - 2):
+                g, h = divmod(i - 2, PAIRS_IN_GROUP)
+                if h == 0:
+                    q_bank = psum_q.tile([P, GROUP, OUT], F32)
+                    q_bank_of[g] = q_bank
+                for a in range(PAIR):
+                    multiply(q_bank_of[g][:, h * PAIR + a, :], cn_mx_of[i - 2], a, wb_codes, wb_scales)
+            if live(i):
+                inv_rms_of[i] = inverse_rms(c_banks_of[i])
+            g, second = divmod(i - 4, PAIRS_IN_GROUP)
+            if 0 <= g < N_GROUPS and second == 0:
+                result_of[g] = rope_straight(q_bank_of[g])
+            if 0 <= g < N_GROUPS and second == 1:
+                rope_crossed(q_bank_of[g], result_of[g], g)
+            if live(i):
+                cn_of[i] = normalise(c_banks_of[i], inv_rms_of[i])
+            if live(i + 2):
+                x_grouped_of[i + 2] = regroup_pair(x_bank_of[i + 2], "x")
+            if live(i - 1):
+                cn_grouped_of[i - 1] = regroup_pair(cn_bank_of[i - 1], "cn")
+
+        for i in range(-2, 0):
+            one_round(i)
+        cos32, sin16 = rope_tables(nc, const, angle)
+        for i in range(0, N_PAIRS + 4):
+            one_round(i)

@@ -239,39 +239,36 @@ def tile_mla_pa_t_kernel(tc, x, wq_a, q_norm_w, wq_b, out):
         cn_of, cn_bank_of, cn_grouped_of, cn_mx_of = {}, {}, {}, {}
         q_bank_of, result_of = {}, {}
         def one_round(i):
+            if live(i + 3):
+                x_grouped_of[i + 3] = regroup_pair(x_bank_of[i + 3], "x")
+            if live(i + 4):
+                x_bank_of[i + 4] = transpose_pair(x_tiles[i + 4][:].bitcast(F32), "x")
+            if live(i + 1):
+                inv_rms_of[i + 1] = inverse_rms(c_banks_of[i + 1])
+            if live(i):
+                cn_of[i] = normalise(c_banks_of[i], inv_rms_of[i])
+                cn_bank_of[i] = transpose_pair(cn_of[i][:].bitcast(F32), "cn")
+                cn_grouped_of[i] = regroup_pair(cn_bank_of[i], "cn")
             if live(i + 2):
-                x_bank_of[i + 2] = transpose_pair(x_tiles[i + 2][:].bitcast(F32), "x")
+                c_banks_of[i + 2] = first_matmul(x_mx_of[i + 2])
             if live(i - 1):
-                cn_bank_of[i - 1] = transpose_pair(cn_of[i - 1][:].bitcast(F32), "cn")
-            if live(i + 1):
-                x_mx_of[i + 1] = quantise_pair(x_grouped_of[i + 1], "x")
-            if live(i - 2):
-                cn_mx_of[i - 2] = quantise_pair(cn_grouped_of[i - 2], "cn")
-            if live(i + 1):
-                c_banks_of[i + 1] = first_matmul(x_mx_of[i + 1])
-            if live(i - 2):
-                g, h = divmod(i - 2, PAIRS_IN_GROUP)
+                cn_mx_of[i - 1] = quantise_pair(cn_grouped_of[i - 1], "cn")
+                g, h = divmod(i - 1, PAIRS_IN_GROUP)
                 if h == 0:
                     q_bank = psum_q.tile([P, GROUP, OUT], F32)
                     q_bank_of[g] = q_bank
                 for a in range(PAIR):
-                    multiply(q_bank_of[g][:, h * PAIR + a, :], cn_mx_of[i - 2], a, wb_codes, wb_scales)
-            if live(i):
-                inv_rms_of[i] = inverse_rms(c_banks_of[i])
-            g, second = divmod(i - 4, PAIRS_IN_GROUP)
+                    multiply(q_bank_of[g][:, h * PAIR + a, :], cn_mx_of[i - 1], a, wb_codes, wb_scales)
+            if live(i + 3):
+                x_mx_of[i + 3] = quantise_pair(x_grouped_of[i + 3], "x")
+            g, second = divmod(i - 3, PAIRS_IN_GROUP)
             if 0 <= g < N_GROUPS and second == 0:
                 result_of[g] = rope_straight(q_bank_of[g])
             if 0 <= g < N_GROUPS and second == 1:
                 rope_crossed(q_bank_of[g], result_of[g], g)
-            if live(i):
-                cn_of[i] = normalise(c_banks_of[i], inv_rms_of[i])
-            if live(i + 2):
-                x_grouped_of[i + 2] = regroup_pair(x_bank_of[i + 2], "x")
-            if live(i - 1):
-                cn_grouped_of[i - 1] = regroup_pair(cn_bank_of[i - 1], "cn")
 
-        for i in range(-2, 0):
+        for i in range(-4, -1):
             one_round(i)
         cos32, sin16 = rope_tables(nc, const, angle)
-        for i in range(0, N_PAIRS + 4):
+        for i in range(-1, N_PAIRS + 3):
             one_round(i)

@@ -186,13 +186,16 @@ def tile_mla_pa_t_kernel(tc, x, wq_a, q_norm_w, wq_b, out):
                 banks.append(c_bank)
             return banks
 
-        def inverse_rms(banks):
+        def square_sums(banks):
             sum_sq = work.tile([P, PAIR], F32)
             for a in range(PAIR):
                 squares = work.tile([P, QL], BF16)
                 nc.scalar.activation(
                     out=squares[:], in_=banks[a][:], func=ACT.Square, accum_out=sum_sq[:, a : a + 1]
                 )
+            return sum_sq
+
+        def inverse_rms(sum_sq):
             inv_rms = work.tile([P, PAIR], F32)
             nc.scalar.activation(
                 out=inv_rms[:], in_=sum_sq[:], func=ACT.Abs_reciprocal_sqrt, scale=1.0 / QL, bias=eps[:]
@@ -237,18 +240,19 @@ def tile_mla_pa_t_kernel(tc, x, wq_a, q_norm_w, wq_b, out):
 
         x_bank_of, x_grouped_of, x_mx_of, c_banks_of, inv_rms_of = {}, {}, {}, {}, {}
         cn_of, cn_bank_of, cn_grouped_of, cn_mx_of = {}, {}, {}, {}
-        q_bank_of, result_of = {}, {}
+        q_bank_of, result_of, sum_sq_of = {}, {}, {}
+
         def one_round(i):
-            if live(i + 3):
-                x_grouped_of[i + 3] = regroup_pair(x_bank_of[i + 3], "x")
-            if live(i + 4):
-                x_bank_of[i + 4] = transpose_pair(x_tiles[i + 4][:].bitcast(F32), "x")
             if live(i + 1):
-                inv_rms_of[i + 1] = inverse_rms(c_banks_of[i + 1])
+                sum_sq_of[i + 1] = square_sums(c_banks_of[i + 1])
             if live(i):
                 cn_of[i] = normalise(c_banks_of[i], inv_rms_of[i])
                 cn_bank_of[i] = transpose_pair(cn_of[i][:].bitcast(F32), "cn")
-                cn_grouped_of[i] = regroup_pair(cn_bank_of[i], "cn")
+            g, second = divmod(i - 3, PAIRS_IN_GROUP)
+            if 0 <= g < N_GROUPS and second == 0:
+                result_of[g] = rope_straight(q_bank_of[g])
+            if 0 <= g < N_GROUPS and second == 1:
+                rope_crossed(q_bank_of[g], result_of[g], g)
             if live(i + 2):
                 c_banks_of[i + 2] = first_matmul(x_mx_of[i + 2])
             if live(i - 1):
@@ -260,12 +264,14 @@ def tile_mla_pa_t_kernel(tc, x, wq_a, q_norm_w, wq_b, out):
                 for a in range(PAIR):
                     multiply(q_bank_of[g][:, h * PAIR + a, :], cn_mx_of[i - 1], a, wb_codes, wb_scales)
             if live(i + 3):
+                x_grouped_of[i + 3] = regroup_pair(x_bank_of[i + 3], "x")
                 x_mx_of[i + 3] = quantise_pair(x_grouped_of[i + 3], "x")
-            g, second = divmod(i - 3, PAIRS_IN_GROUP)
-            if 0 <= g < N_GROUPS and second == 0:
-                result_of[g] = rope_straight(q_bank_of[g])
-            if 0 <= g < N_GROUPS and second == 1:
-                rope_crossed(q_bank_of[g], result_of[g], g)
+            if live(i + 1):
+                inv_rms_of[i + 1] = inverse_rms(sum_sq_of[i + 1])
+            if live(i + 4):
+                x_bank_of[i + 4] = transpose_pair(x_tiles[i + 4][:].bitcast(F32), "x")
+            if live(i):
+                cn_grouped_of[i] = regroup_pair(cn_bank_of[i], "cn")
 
         for i in range(-4, -1):
             one_round(i)

@@ -47,10 +47,17 @@ def load_weight(pool, queue, w, cols, label):
     return raw
 
 
-def regroup_weight(copy, raw, grouped, cols):
+def regroup_wb(copy, raw, grouped):
     copy(
-        out=grouped[:].rearrange("p (c t) -> p c t", t=PACK)[:, cols, :],
-        in_=raw[:].rearrange("p (t c) -> p c t", t=PACK)[:, cols, :],
+        out=grouped[:].rearrange("p (c t) -> p c t", t=PACK),
+        in_=raw[:].rearrange("p (t c) -> p c t", t=PACK),
+    )
+
+
+def regroup_wa(copy, raw, grouped, u):
+    copy(
+        out=grouped[:].rearrange("p (u m e t) -> p u m e t", u=2, e=2, t=PACK)[:, u],
+        in_=raw[:].rearrange("p (t m u e) -> p u m e t", t=PACK, u=2, e=2)[:, u],
     )
 
 
@@ -119,8 +126,11 @@ def tile_mla_pa_t_kernel(tc, x, wq_a, q_norm_w, wq_b, out):
             nc.sync.dma_start(out=x_sb[:], in_=x_groups[g][:, h * PAIR * K : (h + 1) * PAIR * K])
             x_tiles.append(x_sb)
         wb_raw = load_weight(const, nc.scalar, wq_b, OUT, "wb")
-        gain = const.tile([P, QL], BF16)
-        nc.scalar.dma_start(out=gain[:], in_=q_norm_w.partition_broadcast(P))
+        gain_row = const.tile([P, QL], BF16)
+        nc.gpsimd.memset(gain_row[:], 0.0)
+        nc.scalar.dma_start(out=gain_row[0:1, :], in_=q_norm_w.unsqueeze(0))
+        ones = const.tile([P, P], BF16)
+        nc.gpsimd.memset(ones[:], 1.0)
 
         warm = const.tile([P, 1], F32)
         nc.vector.memset(warm[:], 0.0)
@@ -135,9 +145,9 @@ def tile_mla_pa_t_kernel(tc, x, wq_a, q_norm_w, wq_b, out):
         take_off_turns(nc, angle, turns)
         wa_grouped = const.tile([P, QL * PACK], BF16, align_bytes=64)
         wb_grouped = const.tile([P, OUT * PACK], BF16, align_bytes=64)
-        regroup_weight(nc.scalar.copy, wa_raw, wa_grouped, slice(QL // 2, QL))
-        regroup_weight(nc.gpsimd.tensor_copy, wb_raw, wb_grouped, slice(0, OUT))
-        regroup_weight(nc.vector.tensor_copy, wa_raw, wa_grouped, slice(0, QL // 2))
+        regroup_wa(nc.scalar.copy, wa_raw, wa_grouped, 1)
+        regroup_wb(nc.gpsimd.tensor_copy, wb_raw, wb_grouped)
+        regroup_wa(nc.vector.tensor_copy, wa_raw, wa_grouped, 0)
         wa_codes, wa_scales = quantise_weight(nc, const, wa_grouped, QL, "wa")
         take_off_turns(nc, angle, turns)
         wb_codes, wb_scales = quantise_weight(nc, const, wb_grouped, OUT, "wb")
@@ -146,10 +156,14 @@ def tile_mla_pa_t_kernel(tc, x, wq_a, q_norm_w, wq_b, out):
             bank = psum_t.tile([P, PAIR, 2, P], F32, name="%s_bank" % label)
             for a in range(PAIR):
                 for u in range(2):
-                    nc.tensor.transpose(
-                        bank[:, a, u, :], words[:, 2 * a * P + u : 2 * (a + 1) * P : 2], ident[:]
-                    )
+                    nc.tensor.transpose(bank[:, a, u, :], words[:, a, u, :], ident[:])
             return bank
+
+        def x_words(x_sb):
+            return x_sb[:].bitcast(F32).rearrange("q (a p u) -> q a u p", a=PAIR, u=2)
+
+        def cn_words(cn):
+            return cn[:].bitcast(F32).rearrange("q (a u p) -> q a u p", a=PAIR, u=2)
 
         def regroup_pair(bank, label):
             grouped = work.tile([P, PAIR * K], BF16, name="%s_grouped" % label, align_bytes=64)
@@ -247,7 +261,7 @@ def tile_mla_pa_t_kernel(tc, x, wq_a, q_norm_w, wq_b, out):
                 sum_sq_of[i + 1] = square_sums(c_banks_of[i + 1])
             if live(i):
                 cn_of[i] = normalise(c_banks_of[i], inv_rms_of[i])
-                cn_bank_of[i] = transpose_pair(cn_of[i][:].bitcast(F32), "cn")
+                cn_bank_of[i] = transpose_pair(cn_words(cn_of[i]), "cn")
             g, second = divmod(i - 3, PAIRS_IN_GROUP)
             if 0 <= g < N_GROUPS and second == 0:
                 result_of[g] = rope_straight(q_bank_of[g])
@@ -269,12 +283,22 @@ def tile_mla_pa_t_kernel(tc, x, wq_a, q_norm_w, wq_b, out):
             if live(i + 1):
                 inv_rms_of[i + 1] = inverse_rms(sum_sq_of[i + 1])
             if live(i + 4):
-                x_bank_of[i + 4] = transpose_pair(x_tiles[i + 4][:].bitcast(F32), "x")
+                x_bank_of[i + 4] = transpose_pair(x_words(x_tiles[i + 4]), "x")
             if live(i):
                 cn_grouped_of[i] = regroup_pair(cn_bank_of[i], "cn")
 
-        for i in range(-4, -1):
+        one_round(-4)
+        gain_bank = psum_q.tile([P, GROUP, OUT], F32, name="q_bank")
+        nc.tensor.matmul(
+            gain_bank[:].rearrange("p a o -> p (a o)"), lhsT=ones[:], rhs=gain_row[:], start=True, stop=True
+        )
+        for i in range(-3, -1):
             one_round(i)
+        gain = const.tile([P, QL], BF16)
+        nc.scalar.copy(
+            out=gain[:].rearrange("p (u m e) -> p u m e", u=2, e=2),
+            in_=gain_bank[:].rearrange("p a o -> p (a o)").rearrange("p (m u e) -> p u m e", u=2, e=2),
+        )
         cos32, sin16 = rope_tables(nc, const, angle)
         for i in range(-1, N_PAIRS + 3):
             one_round(i)

@@ -35,6 +35,8 @@ TWO_PI_HIGH = 6.28125
 TWO_PI_LOW = TWO_PI - TWO_PI_HIGH
 ROUND_MAGIC = 1.5 * 2.0**23
 
+WARM_COLS = 384
+
 FLOPS = 2 * TOKENS * K * (QL + OUT)
 
 
@@ -152,8 +154,16 @@ def tile_mla_pa_t_kernel(tc, x, wq_a, q_norm_w, wq_b, out):
         take_off_turns(nc, angle, turns)
         wb_codes, wb_scales = quantise_weight(nc, const, wb_grouped, OUT, "wb")
 
-        def transpose_pair(words, label):
+        def transpose_pair(words, label, warm=False):
             bank = psum_t.tile([P, PAIR, 2, P], F32, name="%s_bank" % label)
+            if warm:
+                nc.tensor.matmul(
+                    bank[:].rearrange("p a u t -> p (a u t)")[:, :WARM_COLS],
+                    lhsT=ones[:],
+                    rhs=gain_row[:, :WARM_COLS],
+                    start=True,
+                    stop=True,
+                )
             for a in range(PAIR):
                 for u in range(2):
                     nc.tensor.transpose(bank[:, a, u, :], words[:, a, u, :], ident[:])
@@ -261,7 +271,7 @@ def tile_mla_pa_t_kernel(tc, x, wq_a, q_norm_w, wq_b, out):
                 sum_sq_of[i + 1] = square_sums(c_banks_of[i + 1])
             if live(i):
                 cn_of[i] = normalise(c_banks_of[i], inv_rms_of[i])
-                cn_bank_of[i] = transpose_pair(cn_words(cn_of[i]), "cn")
+                cn_bank_of[i] = transpose_pair(cn_words(cn_of[i]), "cn", warm=True)
             g, second = divmod(i - 3, PAIRS_IN_GROUP)
             if 0 <= g < N_GROUPS and second == 0:
                 result_of[g] = rope_straight(q_bank_of[g])

@@ -28,11 +28,10 @@ PAIR = 2
 N_GROUPS = TOKENS // (GROUP * P)
 PAIRS_IN_GROUP = GROUP // PAIR
 N_PAIRS = N_GROUPS * PAIRS_IN_GROUP
+ROPE_LAG = 3
 VECS = GROUP * OUT // HEAD
 
 TWO_PI = 2.0 * math.pi
-TWO_PI_HIGH = 6.28125
-TWO_PI_LOW = TWO_PI - TWO_PI_HIGH
 ROUND_MAGIC = 1.5 * 2.0**23
 
 WARM_COLS = 384
@@ -56,10 +55,10 @@ def regroup_wb(copy, raw, grouped):
     )
 
 
-def regroup_wa(copy, raw, grouped, u):
+def regroup_wa(copy, raw, grouped, u, m):
     copy(
-        out=grouped[:].rearrange("p (u m e t) -> p u m e t", u=2, e=2, t=PACK)[:, u],
-        in_=raw[:].rearrange("p (t m u e) -> p u m e t", t=PACK, u=2, e=2)[:, u],
+        out=grouped[:].rearrange("p (u m e t) -> p u m e t", u=2, e=2, t=PACK)[:, u, m],
+        in_=raw[:].rearrange("p (t m u e) -> p u m e t", t=PACK, u=2, e=2)[:, u, m],
     )
 
 
@@ -70,40 +69,37 @@ def quantise_weight(nc, pool, grouped, cols, label):
     return codes, scales
 
 
-def rope_angles(nc, pool):
+def rope_turns(nc, pool):
     pos = pool.tile([P, VECS], F32)
     nc.gpsimd.iota(
         pos[:], pattern=[[1, VECS]], base=START, channel_multiplier=VECS, allow_small_or_imprecise_dtypes=True
     )
-    angle = pool.tile([P, 2, VECS, HALF], F32)
+    turns = pool.tile([P, 2, VECS, HALF], F32)
     for j in range(HALF):
-        theta = 10000.0 ** (-j / HALF)
-        nc.vector.tensor_scalar(out=angle[:, 0, :, j], in0=pos[:], scalar1=theta, scalar2=None, op0=ALU.mult)
         nc.vector.tensor_scalar(
-            out=angle[:, 1, :, j], in0=pos[:], scalar1=theta, scalar2=0.5 * math.pi, op0=ALU.mult, op1=ALU.add
+            out=turns[:, 0, :, j], in0=pos[:], scalar1=10000.0 ** (-j / HALF) / TWO_PI, scalar2=None, op0=ALU.mult
         )
-    return angle
-
-
-def take_off_turns(nc, angle, turns):
-    flat = angle[:].rearrange("p s v j -> p (s v j)")
-    nc.vector.tensor_scalar(
-        out=turns[:], in0=flat, scalar1=1.0 / TWO_PI, scalar2=ROUND_MAGIC, op0=ALU.mult, op1=ALU.add
+    nc.vector.tensor_scalar(out=turns[:, 1], in0=turns[:, 0], scalar1=0.25, scalar2=None, op0=ALU.add)
+    whole = pool.tile([P, 2, VECS, HALF], F32)
+    nc.vector.tensor_scalar(out=whole[:], in0=turns[:], scalar1=ROUND_MAGIC, scalar2=None, op0=ALU.add)
+    minus = pool.tile([P, 2, VECS, HALF], F32)
+    nc.vector.scalar_tensor_tensor(
+        out=minus[:], in0=whole[:], scalar=ROUND_MAGIC, in1=turns[:], op0=ALU.subtract, op1=ALU.subtract
     )
-    nc.vector.tensor_scalar(out=turns[:], in0=turns[:], scalar1=ROUND_MAGIC, scalar2=None, op0=ALU.subtract)
-    for part in (TWO_PI_HIGH, TWO_PI_LOW):
-        nc.vector.scalar_tensor_tensor(out=flat, in0=turns[:], scalar=-part, in1=flat, op0=ALU.mult, op1=ALU.add)
+    return minus
 
 
-def rope_tables(nc, pool, angle):
-    cos32 = pool.tile([P, VECS, HEAD], F32)
-    nc.vector.memset(cos32[:], 1.0)
-    nc.scalar.activation(out=cos32[:, :, ROT : ROT + HALF], in_=angle[:, 1], func=ACT.Sin)
-    nc.scalar.activation(out=cos32[:, :, ROT + HALF : HEAD], in_=angle[:, 1], func=ACT.Sin)
-    sin16 = pool.tile([P, VECS, ROT], F32)
-    nc.scalar.activation(out=sin16[:, :, 0:HALF], in_=angle[:, 0], func=ACT.Sin, scale=-1.0)
-    nc.scalar.activation(out=sin16[:, :, HALF:ROT], in_=angle[:, 0], func=ACT.Sin)
-    return cos32, sin16
+def rope_table(nc, pool, minus):
+    trig = pool.tile([P, VECS, 2, ROT], F32)
+    nc.scalar.activation(
+        out=trig[:, :, 0, :].rearrange("p v (s j) -> p v s j", s=2),
+        in_=minus[:, 1].unsqueeze(2).to_broadcast([P, VECS, 2, HALF]),
+        func=ACT.Sin,
+        scale=-TWO_PI,
+    )
+    nc.scalar.activation(out=trig[:, :, 1, 0:HALF], in_=minus[:, 0], func=ACT.Sin, scale=-TWO_PI)
+    nc.scalar.activation(out=trig[:, :, 1, HALF:ROT], in_=minus[:, 0], func=ACT.Sin, scale=TWO_PI)
+    return trig
 
 
 def tile_mla_pa_t_kernel(tc, x, wq_a, q_norm_w, wq_b, out):
@@ -120,39 +116,39 @@ def tile_mla_pa_t_kernel(tc, x, wq_a, q_norm_w, wq_b, out):
         psum_q = ctx.enter_context(tc.psum_pool(name="psum_q", bufs=2))
         ctx.enter_context(tc.manual_schedule())
 
-        wa_raw = load_weight(const, nc.sync, wq_a, QL, "wa")
         x_tiles = []
-        for i in range(N_PAIRS):
+
+        def load_pair(i):
             g, h = divmod(i, PAIRS_IN_GROUP)
             x_sb = x_pool.tile([P, PAIR * K], BF16)
             nc.sync.dma_start(out=x_sb[:], in_=x_groups[g][:, h * PAIR * K : (h + 1) * PAIR * K])
             x_tiles.append(x_sb)
+
+        load_pair(0)
+        wa_raw = load_weight(const, nc.sync, wq_a, QL, "wa")
         wb_raw = load_weight(const, nc.scalar, wq_b, OUT, "wb")
+        load_pair(1)
         gain_row = const.tile([P, QL], BF16)
-        nc.gpsimd.memset(gain_row[:], 0.0)
-        nc.scalar.dma_start(out=gain_row[0:1, :], in_=q_norm_w.unsqueeze(0))
-        ones = const.tile([P, P], BF16)
-        nc.gpsimd.memset(ones[:], 1.0)
+        nc.vector.memset(gain_row[:], 0.0)
+        nc.sync.dma_start(out=gain_row[0:1, :], in_=q_norm_w.unsqueeze(0))
+        for i in range(2, N_PAIRS):
+            load_pair(i)
 
         warm = const.tile([P, 1], F32)
         nc.vector.memset(warm[:], 0.0)
         nc.scalar.activation(out=warm[:], in_=warm[:], func=ACT.Sin)
-
-        ident = const.tile([P, P], F32)
-        make_identity(nc, ident[:])
         eps = const.tile([P, 1], F32)
         nc.vector.memset(eps[:], EPS)
-        angle = rope_angles(nc, const)
-        turns = const.tile([P, 2 * VECS * HALF], F32)
-        take_off_turns(nc, angle, turns)
+        minus = rope_turns(nc, const)
+        ident = const.tile([P, P], F32)
+        make_identity(nc, ident[:])
+        ones = const.tile([P, P], BF16)
+        nc.gpsimd.memset(ones[:], 1.0)
+        trig = rope_table(nc, const, minus)
+        nc.scalar.activation(out=warm[:], in_=eps[:], func=ACT.Abs_reciprocal_sqrt)
         wa_grouped = const.tile([P, QL * PACK], BF16, align_bytes=64)
         wb_grouped = const.tile([P, OUT * PACK], BF16, align_bytes=64)
-        regroup_wa(nc.scalar.copy, wa_raw, wa_grouped, 1)
         regroup_wb(nc.gpsimd.tensor_copy, wb_raw, wb_grouped)
-        regroup_wa(nc.vector.tensor_copy, wa_raw, wa_grouped, 0)
-        wa_codes, wa_scales = quantise_weight(nc, const, wa_grouped, QL, "wa")
-        take_off_turns(nc, angle, turns)
-        wb_codes, wb_scales = quantise_weight(nc, const, wb_grouped, OUT, "wb")
 
         def transpose_pair(words, label, warm=False):
             bank = psum_t.tile([P, PAIR, 2, P], F32, name="%s_bank" % label)
@@ -175,19 +171,35 @@ def tile_mla_pa_t_kernel(tc, x, wq_a, q_norm_w, wq_b, out):
         def cn_words(cn):
             return cn[:].bitcast(F32).rearrange("q (a u p) -> q a u p", a=PAIR, u=2)
 
-        def regroup_pair(bank, label):
-            grouped = work.tile([P, PAIR * K], BF16, name="%s_grouped" % label, align_bytes=64)
-            nc.scalar.copy(
-                out=grouped[:].bitcast(F32).rearrange("p (a t u) -> p a t u", a=PAIR, u=2),
-                in_=bank[:].rearrange("p a u t -> p a t u"),
+        def regroup(bank, grouped, tiles, copy):
+            copy(
+                out=grouped[:].bitcast(F32).rearrange("p (a t u) -> p a t u", a=PAIR, u=2)[:, tiles],
+                in_=bank[:, tiles].rearrange("p a u t -> p a t u"),
             )
+
+        def regroup_pair(bank, label, copy=nc.scalar.copy):
+            grouped = work.tile([P, PAIR * K], BF16, name="%s_grouped" % label, align_bytes=64)
+            regroup(bank, grouped, slice(0, PAIR), copy)
             return grouped
 
-        def quantise_pair(grouped, label):
+        def quantise(grouped, operand, tiles):
+            codes, scales = operand
+            words = slice(tiles.start * P, tiles.stop * P)
+            nc.vector.quantize_mx(
+                out=codes[:, words].bitcast(FP8X4),
+                scales=scales[:, words],
+                in_=grouped[:, tiles.start * K : tiles.stop * K],
+            )
+
+        def new_operand(label):
             codes = work.tile([P, PAIR * P], U32, name="%s_codes" % label, align_bytes=64)
             scales = work.tile([P, PAIR * P], U8, name="%s_scales" % label, align_bytes=64)
-            nc.vector.quantize_mx(out=codes[:].bitcast(FP8X4), scales=scales[:], in_=grouped[:])
             return codes, scales
+
+        def quantise_pair(grouped, label):
+            operand = new_operand(label)
+            quantise(grouped, operand, slice(0, PAIR))
+            return operand
 
         def multiply(acc, operand, a, w_codes, w_scales):
             codes, scales = operand
@@ -239,76 +251,124 @@ def tile_mla_pa_t_kernel(tc, x, wq_a, q_norm_w, wq_b, out):
                 )
             return cn
 
-        def rope_straight(q_bank):
-            result = work.tile([P, VECS, HEAD], F32)
+        def rope_products(q_bank, vecs):
+            n = vecs.stop - vecs.start
             q = q_bank[:].rearrange("p a (h d) -> p (a h) d", d=HEAD)
-            nc.vector.tensor_tensor(out=result[:], in0=q, in1=cos32[:], op=ALU.mult)
+            products = work.tile([P, VECS, 2, ROT], F32)
+            nc.vector.tensor_tensor(
+                out=products[:, vecs],
+                in0=q[:, vecs, ROT:HEAD].unsqueeze(2).to_broadcast([P, n, 2, ROT]),
+                in1=trig[:, vecs],
+                op=ALU.mult,
+            )
+            return products
+
+        def plain_values(q_bank, vecs, copy):
+            q = q_bank[:].rearrange("p a (h d) -> p (a h) d", d=HEAD)
+            result = work.tile([P, VECS, HEAD], F32)
+            copy(out=result[:, vecs, 0:ROT], in_=q[:, vecs, 0:ROT])
             return result
 
-        def rope_crossed(q_bank, result, g):
-            q = q_bank[:].rearrange("p a (h d) -> p (a h) d", d=HEAD)
-            crossed = work.tile([P, VECS, ROT], F32)
+        def rope_sum(products, result, g, vecs):
+            by_half = products[:, vecs].rearrange("p v x (s j) -> p v x s j", s=2)
             nc.vector.tensor_tensor(
-                out=crossed[:, :, 0:HALF], in0=q[:, :, ROT + HALF : HEAD], in1=sin16[:, :, 0:HALF], op=ALU.mult
+                out=result[:, vecs, ROT:HEAD].rearrange("p v (s j) -> p v s j", s=2),
+                in0=by_half[:, :, 0],
+                in1=by_half[:, :, 1, ::-1, :],
+                op=ALU.add,
             )
-            nc.vector.tensor_tensor(
-                out=crossed[:, :, HALF:ROT], in0=q[:, :, ROT : ROT + HALF], in1=sin16[:, :, HALF:ROT], op=ALU.mult
+            nc.sync.dma_start(
+                out=out_groups[g][:, vecs.start * HEAD : vecs.stop * HEAD],
+                in_=result[:, vecs].rearrange("p v d -> p (v d)"),
             )
-            nc.vector.tensor_tensor(
-                out=result[:, :, ROT:HEAD], in0=result[:, :, ROT:HEAD], in1=crossed[:], op=ALU.add
-            )
-            nc.sync.dma_start(out=out_groups[g], in_=result[:].rearrange("p v d -> p (v d)"))
 
         def live(i):
             return 0 <= i < N_PAIRS
 
         x_bank_of, x_grouped_of, x_mx_of, c_banks_of, inv_rms_of = {}, {}, {}, {}, {}
         cn_of, cn_bank_of, cn_grouped_of, cn_mx_of = {}, {}, {}, {}
-        q_bank_of, result_of, sum_sq_of = {}, {}, {}
+        q_bank_of, products_of, sum_sq_of = {}, {}, {}
+        all_vecs = slice(0, VECS)
 
-        def one_round(i):
+        def second_matmul(i, tiles):
+            g, h = divmod(i, PAIRS_IN_GROUP)
+            if h == 0 and tiles.start == 0:
+                q_bank = psum_q.tile([P, GROUP, OUT], F32)
+                q_bank_of[g] = q_bank
+            for a in range(tiles.start, tiles.stop):
+                multiply(q_bank_of[g][:, h * PAIR + a, :], cn_mx_of[i], a, wb_codes, wb_scales)
+
+        def one_round(i, vector_copies_x):
             if live(i + 1):
                 sum_sq_of[i + 1] = square_sums(c_banks_of[i + 1])
+                if vector_copies_x:
+                    inv_rms_of[i + 1] = inverse_rms(sum_sq_of[i + 1])
             if live(i):
                 cn_of[i] = normalise(c_banks_of[i], inv_rms_of[i])
                 cn_bank_of[i] = transpose_pair(cn_words(cn_of[i]), "cn", warm=True)
-            g, second = divmod(i - 3, PAIRS_IN_GROUP)
-            if 0 <= g < N_GROUPS and second == 0:
-                result_of[g] = rope_straight(q_bank_of[g])
-            if 0 <= g < N_GROUPS and second == 1:
-                rope_crossed(q_bank_of[g], result_of[g], g)
+            g, second = divmod(i - ROPE_LAG, PAIRS_IN_GROUP)
+            if g >= 0 and second == 0:
+                products_of[g] = rope_products(q_bank_of[g], all_vecs)
+            if g >= 0 and second == 1:
+                result = plain_values(q_bank_of[g], all_vecs, nc.vector.tensor_copy)
+                rope_sum(products_of[g], result, g, all_vecs)
             if live(i + 2):
                 c_banks_of[i + 2] = first_matmul(x_mx_of[i + 2])
+            if vector_copies_x:
+                x_grouped_of[i + 3] = regroup_pair(x_bank_of[i + 3], "x", nc.vector.tensor_copy)
             if live(i - 1):
                 cn_mx_of[i - 1] = quantise_pair(cn_grouped_of[i - 1], "cn")
-                g, h = divmod(i - 1, PAIRS_IN_GROUP)
-                if h == 0:
-                    q_bank = psum_q.tile([P, GROUP, OUT], F32)
-                    q_bank_of[g] = q_bank
-                for a in range(PAIR):
-                    multiply(q_bank_of[g][:, h * PAIR + a, :], cn_mx_of[i - 1], a, wb_codes, wb_scales)
+                second_matmul(i - 1, slice(0, PAIR))
             if live(i + 3):
-                x_grouped_of[i + 3] = regroup_pair(x_bank_of[i + 3], "x")
+                if not vector_copies_x:
+                    x_grouped_of[i + 3] = regroup_pair(x_bank_of[i + 3], "x")
                 x_mx_of[i + 3] = quantise_pair(x_grouped_of[i + 3], "x")
-            if live(i + 1):
+            if live(i + 1) and not vector_copies_x:
                 inv_rms_of[i + 1] = inverse_rms(sum_sq_of[i + 1])
             if live(i + 4):
                 x_bank_of[i + 4] = transpose_pair(x_words(x_tiles[i + 4]), "x")
             if live(i):
                 cn_grouped_of[i] = regroup_pair(cn_bank_of[i], "cn")
 
-        one_round(-4)
+        x_bank_of[0] = transpose_pair(x_words(x_tiles[0]), "x")
+        x_grouped_of[0] = regroup_pair(x_bank_of[0], "x", nc.vector.tensor_copy)
+        x_bank_of[1] = transpose_pair(x_words(x_tiles[1]), "x")
+        regroup_wa(nc.scalar.copy, wa_raw, wa_grouped, 1, slice(P // 2, P))
+        regroup_wa(nc.vector.tensor_copy, wa_raw, wa_grouped, 0, slice(0, P))
+        regroup_wa(nc.vector.tensor_copy, wa_raw, wa_grouped, 1, slice(0, P // 2))
+        x_mx_of[0] = quantise_pair(x_grouped_of[0], "x")
+        wa_codes, wa_scales = quantise_weight(nc, const, wa_grouped, QL, "wa")
         gain_bank = psum_q.tile([P, GROUP, OUT], F32, name="q_bank")
         nc.tensor.matmul(
             gain_bank[:].rearrange("p a o -> p (a o)"), lhsT=ones[:], rhs=gain_row[:], start=True, stop=True
         )
-        for i in range(-3, -1):
-            one_round(i)
+        one_round(-2, False)
+        wb_codes, wb_scales = quantise_weight(nc, const, wb_grouped, OUT, "wb")
         gain = const.tile([P, QL], BF16)
         nc.scalar.copy(
             out=gain[:].rearrange("p (u m e) -> p u m e", u=2, e=2),
             in_=gain_bank[:].rearrange("p a o -> p (a o)").rearrange("p (m u e) -> p u m e", u=2, e=2),
         )
-        cos32, sin16 = rope_tables(nc, const, angle)
-        for i in range(-1, N_PAIRS + 3):
-            one_round(i)
+        for i in range(-1, N_PAIRS - 1):
+            one_round(i, i < ROPE_LAG)
+
+        last = N_PAIRS - 1
+        g = N_GROUPS - 1
+        cn_of[last] = normalise(c_banks_of[last], inv_rms_of[last])
+        cn_bank_of[last] = transpose_pair(cn_words(cn_of[last]), "cn")
+        products_of[g - 1] = rope_products(q_bank_of[g - 1], all_vecs)
+        cn_mx_of[last - 1] = quantise_pair(cn_grouped_of[last - 1], "cn")
+        second_matmul(last - 1, slice(0, PAIR))
+        cn_grouped = work.tile([P, PAIR * K], BF16, align_bytes=64)
+        cn_mx_of[last] = new_operand("cn")
+        for a in range(PAIR):
+            regroup(cn_bank_of[last], cn_grouped, slice(a, a + 1), nc.scalar.copy)
+            quantise(cn_grouped, cn_mx_of[last], slice(a, a + 1))
+            second_matmul(last, slice(a, a + 1))
+        result = plain_values(q_bank_of[g - 1], all_vecs, nc.scalar.copy)
+        rope_sum(products_of[g - 1], result, g - 1, all_vecs)
+        halves = [slice(0, VECS // 2), slice(VECS // 2, VECS)]
+        results = [plain_values(q_bank_of[g], half, nc.scalar.copy) for half in halves]
+        products = [rope_products(q_bank_of[g], half) for half in halves]
+        for half in range(2):
+            rope_sum(products[half], results[half], g, halves[half])

@@ -28,6 +28,7 @@ PAIR = 2
 N_GROUPS = TOKENS // (GROUP * P)
 PAIRS_IN_GROUP = GROUP // PAIR
 N_PAIRS = N_GROUPS * PAIRS_IN_GROUP
+X_LEAD = 3
 ROPE_LAG = 3
 VECS = GROUP * OUT // HEAD
 
@@ -171,35 +172,30 @@ def tile_mla_pa_t_kernel(tc, x, wq_a, q_norm_w, wq_b, out):
         def cn_words(cn):
             return cn[:].bitcast(F32).rearrange("q (a u p) -> q a u p", a=PAIR, u=2)
 
-        def regroup(bank, grouped, tiles, copy):
+        X, CN = 0, 1
+        grouped_of, mx_of = {}, {}
+
+        def regroup(bank, i, part, tiles, copy):
+            if i not in grouped_of:
+                grouped = work.tile([P, 2 * PAIR * K], BF16, align_bytes=64)
+                grouped_of[i] = grouped
             copy(
-                out=grouped[:].bitcast(F32).rearrange("p (a t u) -> p a t u", a=PAIR, u=2)[:, tiles],
+                out=grouped_of[i][:].bitcast(F32).rearrange("p (x a t u) -> p x a t u", x=2, a=PAIR, u=2)[:, part, tiles],
                 in_=bank[:, tiles].rearrange("p a u t -> p a t u"),
             )
 
-        def regroup_pair(bank, label, copy=nc.scalar.copy):
-            grouped = work.tile([P, PAIR * K], BF16, name="%s_grouped" % label, align_bytes=64)
-            regroup(bank, grouped, slice(0, PAIR), copy)
-            return grouped
-
-        def quantise(grouped, operand, tiles):
-            codes, scales = operand
-            words = slice(tiles.start * P, tiles.stop * P)
+        def quantise(i, first, count):
+            if i not in mx_of:
+                codes = work.tile([P, 2 * PAIR * P], U32, align_bytes=64)
+                scales = work.tile([P, 2 * PAIR * P], U8, align_bytes=64)
+                mx_of[i] = (codes, scales)
+            codes, scales = mx_of[i]
+            words = slice(first * P, (first + count) * P)
             nc.vector.quantize_mx(
                 out=codes[:, words].bitcast(FP8X4),
                 scales=scales[:, words],
-                in_=grouped[:, tiles.start * K : tiles.stop * K],
+                in_=grouped_of[i][:, first * K : (first + count) * K],
             )
-
-        def new_operand(label):
-            codes = work.tile([P, PAIR * P], U32, name="%s_codes" % label, align_bytes=64)
-            scales = work.tile([P, PAIR * P], U8, name="%s_scales" % label, align_bytes=64)
-            return codes, scales
-
-        def quantise_pair(grouped, label):
-            operand = new_operand(label)
-            quantise(grouped, operand, slice(0, PAIR))
-            return operand
 
         def multiply(acc, operand, a, w_codes, w_scales):
             codes, scales = operand
@@ -214,11 +210,11 @@ def tile_mla_pa_t_kernel(tc, x, wq_a, q_norm_w, wq_b, out):
                 stop=True,
             )
 
-        def first_matmul(operand):
+        def first_matmul(i):
             banks = []
             for a in range(PAIR):
                 c_bank = psum_c.tile([P, QL], F32)
-                multiply(c_bank[:], operand, a, wa_codes, wa_scales)
+                multiply(c_bank[:], mx_of[i - X_LEAD], a, wa_codes, wa_scales)
                 banks.append(c_bank)
             return banks
 
@@ -285,18 +281,15 @@ def tile_mla_pa_t_kernel(tc, x, wq_a, q_norm_w, wq_b, out):
         def live(i):
             return 0 <= i < N_PAIRS
 
-        x_bank_of, x_grouped_of, x_mx_of, c_banks_of, inv_rms_of = {}, {}, {}, {}, {}
-        cn_of, cn_bank_of, cn_grouped_of, cn_mx_of = {}, {}, {}, {}
+        x_bank_of, c_banks_of, inv_rms_of, cn_of, cn_bank_of = {}, {}, {}, {}, {}
         q_bank_of, products_of, sum_sq_of = {}, {}, {}
         all_vecs = slice(0, VECS)
+        both = slice(0, PAIR)
 
-        def second_matmul(i, tiles):
-            g, h = divmod(i, PAIRS_IN_GROUP)
-            if h == 0 and tiles.start == 0:
-                q_bank = psum_q.tile([P, GROUP, OUT], F32)
-                q_bank_of[g] = q_bank
+        def second_matmul(i, q_bank, tiles):
+            h = i % PAIRS_IN_GROUP
             for a in range(tiles.start, tiles.stop):
-                multiply(q_bank_of[g][:, h * PAIR + a, :], cn_mx_of[i], a, wb_codes, wb_scales)
+                multiply(q_bank[:, h * PAIR + a, :], mx_of[i + 1], PAIR + a, wb_codes, wb_scales)
 
         def one_round(i, vector_copies_x):
             if live(i + 1):
@@ -313,36 +306,40 @@ def tile_mla_pa_t_kernel(tc, x, wq_a, q_norm_w, wq_b, out):
                 result = plain_values(q_bank_of[g], all_vecs, nc.vector.tensor_copy)
                 rope_sum(products_of[g], result, g, all_vecs)
             if live(i + 2):
-                c_banks_of[i + 2] = first_matmul(x_mx_of[i + 2])
-            if vector_copies_x:
-                x_grouped_of[i + 3] = regroup_pair(x_bank_of[i + 3], "x", nc.vector.tensor_copy)
-            if live(i - 1):
-                cn_mx_of[i - 1] = quantise_pair(cn_grouped_of[i - 1], "cn")
-                second_matmul(i - 1, slice(0, PAIR))
-            if live(i + 3):
-                if not vector_copies_x:
-                    x_grouped_of[i + 3] = regroup_pair(x_bank_of[i + 3], "x")
-                x_mx_of[i + 3] = quantise_pair(x_grouped_of[i + 3], "x")
+                c_banks_of[i + 2] = first_matmul(i + 2)
+            with_x, with_cn = live(i + X_LEAD), live(i - 1)
+            quantise(i, X if with_x else PAIR, PAIR * (with_x + with_cn))
+            if with_cn:
+                g, h = divmod(i - 1, PAIRS_IN_GROUP)
+                if h == 0:
+                    q_bank = psum_q.tile([P, GROUP, OUT], F32)
+                    q_bank_of[g] = q_bank
+                second_matmul(i - 1, q_bank_of[g], both)
+            if live(i + 1 + X_LEAD):
+                copy = nc.vector.tensor_copy if vector_copies_x else nc.scalar.copy
+                regroup(x_bank_of[i + 1 + X_LEAD], i + 1, X, both, copy)
             if live(i + 1) and not vector_copies_x:
                 inv_rms_of[i + 1] = inverse_rms(sum_sq_of[i + 1])
-            if live(i + 4):
-                x_bank_of[i + 4] = transpose_pair(x_words(x_tiles[i + 4]), "x")
+            if live(i + 2 + X_LEAD):
+                x_bank_of[i + 2 + X_LEAD] = transpose_pair(x_words(x_tiles[i + 2 + X_LEAD]), "x")
             if live(i):
-                cn_grouped_of[i] = regroup_pair(cn_bank_of[i], "cn")
+                regroup(cn_bank_of[i], i + 1, CN, both, nc.scalar.copy)
 
         x_bank_of[0] = transpose_pair(x_words(x_tiles[0]), "x")
-        x_grouped_of[0] = regroup_pair(x_bank_of[0], "x", nc.vector.tensor_copy)
+        regroup(x_bank_of[0], -X_LEAD, X, both, nc.vector.tensor_copy)
         x_bank_of[1] = transpose_pair(x_words(x_tiles[1]), "x")
         regroup_wa(nc.scalar.copy, wa_raw, wa_grouped, 1, slice(P // 2, P))
         regroup_wa(nc.vector.tensor_copy, wa_raw, wa_grouped, 0, slice(0, P))
         regroup_wa(nc.vector.tensor_copy, wa_raw, wa_grouped, 1, slice(0, P // 2))
-        x_mx_of[0] = quantise_pair(x_grouped_of[0], "x")
+        quantise(-X_LEAD, X, PAIR)
         wa_codes, wa_scales = quantise_weight(nc, const, wa_grouped, QL, "wa")
         gain_bank = psum_q.tile([P, GROUP, OUT], F32, name="q_bank")
         nc.tensor.matmul(
             gain_bank[:].rearrange("p a o -> p (a o)"), lhsT=ones[:], rhs=gain_row[:], start=True, stop=True
         )
-        one_round(-2, False)
+        regroup(x_bank_of[1], 1 - X_LEAD, X, both, nc.scalar.copy)
+        x_bank_of[2] = transpose_pair(x_words(x_tiles[2]), "x")
+        one_round(-2, True)
         wb_codes, wb_scales = quantise_weight(nc, const, wb_grouped, OUT, "wb")
         gain = const.tile([P, QL], BF16)
         nc.scalar.copy(
@@ -354,21 +351,26 @@ def tile_mla_pa_t_kernel(tc, x, wq_a, q_norm_w, wq_b, out):
 
         last = N_PAIRS - 1
         g = N_GROUPS - 1
+        halves = [slice(0, VECS // 2), slice(VECS // 2, VECS)]
         cn_of[last] = normalise(c_banks_of[last], inv_rms_of[last])
         cn_bank_of[last] = transpose_pair(cn_words(cn_of[last]), "cn")
-        products_of[g - 1] = rope_products(q_bank_of[g - 1], all_vecs)
-        cn_mx_of[last - 1] = quantise_pair(cn_grouped_of[last - 1], "cn")
-        second_matmul(last - 1, slice(0, PAIR))
-        cn_grouped = work.tile([P, PAIR * K], BF16, align_bytes=64)
-        cn_mx_of[last] = new_operand("cn")
-        for a in range(PAIR):
-            regroup(cn_bank_of[last], cn_grouped, slice(a, a + 1), nc.scalar.copy)
-            quantise(cn_grouped, cn_mx_of[last], slice(a, a + 1))
-            second_matmul(last, slice(a, a + 1))
         result = plain_values(q_bank_of[g - 1], all_vecs, nc.scalar.copy)
+        products_of[g - 1] = rope_products(q_bank_of[g - 1], all_vecs)
+        q_banks = []
+        for half in halves:
+            q_bank = psum_q.tile([P, GROUP, OUT], F32)
+            q_banks.append(q_bank)
+        quantise(last, PAIR, PAIR)
+        second_matmul(last - 1, q_banks[0], both)
+        for a in range(PAIR):
+            tile = slice(a, a + 1)
+            regroup(cn_bank_of[last], N_PAIRS, CN, tile, nc.scalar.copy)
+            quantise(N_PAIRS, PAIR + a, 1)
+            second_matmul(last, q_banks[1], tile)
         rope_sum(products_of[g - 1], result, g - 1, all_vecs)
-        halves = [slice(0, VECS // 2), slice(VECS // 2, VECS)]
-        results = [plain_values(q_bank_of[g], half, nc.scalar.copy) for half in halves]
-        products = [rope_products(q_bank_of[g], half) for half in halves]
-        for half in range(2):
-            rope_sum(products[half], results[half], g, halves[half])
+        first_result = plain_values(q_banks[0], halves[0], nc.scalar.copy)
+        first_products = rope_products(q_banks[0], halves[0])
+        second_products = rope_products(q_banks[1], halves[1])
+        second_result = plain_values(q_banks[1], halves[1], nc.scalar.copy)
+        rope_sum(first_products, first_result, g, halves[0])
+        rope_sum(second_products, second_result, g, halves[1])

import math
from contextlib import ExitStack

import concourse.mybir as mybir
from concourse.masks import make_identity

F32 = mybir.dt.float32
BF16 = mybir.dt.bfloat16
U32 = mybir.dt.uint32
U8 = mybir.dt.uint8
FP8X4 = mybir.dt.float8_e4m3fn_x4
ALU = mybir.AluOpType
ACT = mybir.ActivationFunctionType

P = 128
PACK = 4
K = P * PACK
TOKENS = 4 * 2048
QL = 512
OUT = 128
HEAD = 32
ROT = 16
HALF = ROT // 2
START = 37
EPS = 1e-6
GROUP = 4
PAIR = 2
N_GROUPS = TOKENS // (GROUP * P)
PAIRS_IN_GROUP = GROUP // PAIR
N_PAIRS = N_GROUPS * PAIRS_IN_GROUP
X_LEAD = 3
ROPE_LAG = 3
VECS = GROUP * OUT // HEAD

TWO_PI = 2.0 * math.pi
ROUND_MAGIC = 1.5 * 2.0**23

WARM_COLS = 384

FLOPS = 2 * TOKENS * K * (QL + OUT)


def load_weight(pool, queue, w, cols, label):
    raw = pool.tile([P, PACK * cols], BF16, name="%s_raw" % label)
    queue.dma_start(
        out=raw[:],
        in_=w.rearrange("(p t) c -> p (t c)", p=P),
    )
    return raw


def regroup_wb(copy, raw, grouped):
    copy(
        out=grouped[:].rearrange("p (c t) -> p c t", t=PACK),
        in_=raw[:].rearrange("p (t c) -> p c t", t=PACK),
    )


def regroup_wa(copy, raw, grouped, u, m):
    copy(
        out=grouped[:].rearrange("p (u m e t) -> p u m e t", u=2, e=2, t=PACK)[:, u, m],
        in_=raw[:].rearrange("p (t m u e) -> p u m e t", t=PACK, u=2, e=2)[:, u, m],
    )


def quantise_weight(nc, pool, grouped, cols, label):
    codes = pool.tile([P, cols], U32, name="%s_codes" % label, align_bytes=64)
    scales = pool.tile([P, cols], U8, name="%s_scales" % label, align_bytes=64)
    nc.vector.quantize_mx(out=codes[:].bitcast(FP8X4), scales=scales[:], in_=grouped[:])
    return codes, scales


def rope_turns(nc, pool):
    pos = pool.tile([P, VECS], F32)
    nc.gpsimd.iota(
        pos[:], pattern=[[1, VECS]], base=START, channel_multiplier=VECS, allow_small_or_imprecise_dtypes=True
    )
    turns = pool.tile([P, 2, VECS, HALF], F32)
    for j in range(HALF):
        nc.vector.tensor_scalar(
            out=turns[:, 0, :, j], in0=pos[:], scalar1=10000.0 ** (-j / HALF) / TWO_PI, scalar2=None, op0=ALU.mult
        )
    nc.vector.tensor_scalar(out=turns[:, 1], in0=turns[:, 0], scalar1=0.25, scalar2=None, op0=ALU.add)
    whole = pool.tile([P, 2, VECS, HALF], F32)
    nc.vector.tensor_scalar(out=whole[:], in0=turns[:], scalar1=ROUND_MAGIC, scalar2=None, op0=ALU.add)
    minus = pool.tile([P, 2, VECS, HALF], F32)
    nc.vector.scalar_tensor_tensor(
        out=minus[:], in0=whole[:], scalar=ROUND_MAGIC, in1=turns[:], op0=ALU.subtract, op1=ALU.subtract
    )
    return minus


def rope_table(nc, pool, minus):
    trig = pool.tile([P, VECS, 2, ROT], F32)
    nc.scalar.activation(
        out=trig[:, :, 0, :].rearrange("p v (s j) -> p v s j", s=2),
        in_=minus[:, 1].unsqueeze(2).to_broadcast([P, VECS, 2, HALF]),
        func=ACT.Sin,
        scale=-TWO_PI,
    )
    nc.scalar.activation(out=trig[:, :, 1, 0:HALF], in_=minus[:, 0], func=ACT.Sin, scale=-TWO_PI)
    nc.scalar.activation(out=trig[:, :, 1, HALF:ROT], in_=minus[:, 0], func=ACT.Sin, scale=TWO_PI)
    return trig


def tile_mla_pa_t_kernel(tc, x, wq_a, q_norm_w, wq_b, out):
    nc = tc.nc
    x_groups = x.rearrange("b (c p a) k -> (b c) p (a k)", p=P, a=GROUP)
    out_groups = out.rearrange("b (c p a) h d -> (b c) p (a h d)", p=P, a=GROUP)

    with ExitStack() as ctx:
        const = ctx.enter_context(tc.tile_pool(name="const", bufs=1))
        x_pool = ctx.enter_context(tc.tile_pool(name="x_pool", bufs=N_PAIRS))
        work = ctx.enter_context(tc.tile_pool(name="work", bufs=3))
        psum_t = ctx.enter_context(tc.psum_pool(name="psum_t", bufs=1))
        psum_c = ctx.enter_context(tc.psum_pool(name="psum_c", bufs=4))
        psum_q = ctx.enter_context(tc.psum_pool(name="psum_q", bufs=2))
        ctx.enter_context(tc.manual_schedule())

        x_tiles = []

        def load_pair(i):
            g, h = divmod(i, PAIRS_IN_GROUP)
            x_sb = x_pool.tile([P, PAIR * K], BF16)
            nc.sync.dma_start(out=x_sb[:], in_=x_groups[g][:, h * PAIR * K : (h + 1) * PAIR * K])
            x_tiles.append(x_sb)

        load_pair(0)
        wa_raw = load_weight(const, nc.sync, wq_a, QL, "wa")
        wb_raw = load_weight(const, nc.scalar, wq_b, OUT, "wb")
        load_pair(1)
        gain_row = const.tile([P, QL], BF16)
        nc.vector.memset(gain_row[:], 0.0)
        nc.sync.dma_start(out=gain_row[0:1, :], in_=q_norm_w.unsqueeze(0))
        for i in range(2, N_PAIRS):
            load_pair(i)

        warm = const.tile([P, 1], F32)
        nc.vector.memset(warm[:], 0.0)
        nc.scalar.activation(out=warm[:], in_=warm[:], func=ACT.Sin)
        eps = const.tile([P, 1], F32)
        nc.vector.memset(eps[:], EPS)
        minus = rope_turns(nc, const)
        ident = const.tile([P, P], F32)
        make_identity(nc, ident[:])
        ones = const.tile([P, P], BF16)
        nc.gpsimd.memset(ones[:], 1.0)
        trig = rope_table(nc, const, minus)
        nc.scalar.activation(out=warm[:], in_=eps[:], func=ACT.Abs_reciprocal_sqrt)
        wa_grouped = const.tile([P, QL * PACK], BF16, align_bytes=64)
        wb_grouped = const.tile([P, OUT * PACK], BF16, align_bytes=64)
        regroup_wb(nc.gpsimd.tensor_copy, wb_raw, wb_grouped)

        def transpose_pair(words, label, warm=False):
            bank = psum_t.tile([P, PAIR, 2, P], F32, name="%s_bank" % label)
            if warm:
                nc.tensor.matmul(
                    bank[:].rearrange("p a u t -> p (a u t)")[:, :WARM_COLS],
                    lhsT=ones[:],
                    rhs=gain_row[:, :WARM_COLS],
                    start=True,
                    stop=True,
                )
            for a in range(PAIR):
                for u in range(2):
                    nc.tensor.transpose(bank[:, a, u, :], words[:, a, u, :], ident[:])
            return bank

        def x_words(x_sb):
            return x_sb[:].bitcast(F32).rearrange("q (a p u) -> q a u p", a=PAIR, u=2)

        def cn_words(cn):
            return cn[:].bitcast(F32).rearrange("q (a u p) -> q a u p", a=PAIR, u=2)

        X, CN = 0, 1
        grouped_of, mx_of = {}, {}

        def regroup(bank, i, part, tiles, copy):
            if i not in grouped_of:
                grouped = work.tile([P, 2 * PAIR * K], BF16, align_bytes=64)
                grouped_of[i] = grouped
            copy(
                out=grouped_of[i][:].bitcast(F32).rearrange("p (x a t u) -> p x a t u", x=2, a=PAIR, u=2)[:, part, tiles],
                in_=bank[:, tiles].rearrange("p a u t -> p a t u"),
            )

        def quantise(i, first, count):
            if i not in mx_of:
                codes = work.tile([P, 2 * PAIR * P], U32, align_bytes=64)
                scales = work.tile([P, 2 * PAIR * P], U8, align_bytes=64)
                mx_of[i] = (codes, scales)
            codes, scales = mx_of[i]
            words = slice(first * P, (first + count) * P)
            nc.vector.quantize_mx(
                out=codes[:, words].bitcast(FP8X4),
                scales=scales[:, words],
                in_=grouped_of[i][:, first * K : (first + count) * K],
            )

        def multiply(acc, operand, a, w_codes, w_scales):
            codes, scales = operand
            tokens = slice(a * P, (a + 1) * P)
            nc.tensor.matmul_mx(
                out=acc,
                lhsT=codes[:, tokens].bitcast(FP8X4),
                lhsT_scale=scales[:, tokens],
                rhs=w_codes[:].bitcast(FP8X4),
                rhs_scale=w_scales[:],
                start=True,
                stop=True,
            )

        def first_matmul(i):
            banks = []
            for a in range(PAIR):
                c_bank = psum_c.tile([P, QL], F32)
                multiply(c_bank[:], mx_of[i - X_LEAD], a, wa_codes, wa_scales)
                banks.append(c_bank)
            return banks

        def square_sums(banks):
            sum_sq = work.tile([P, PAIR], F32)
            for a in range(PAIR):
                squares = work.tile([P, QL], BF16)
                nc.scalar.activation(
                    out=squares[:], in_=banks[a][:], func=ACT.Square, accum_out=sum_sq[:, a : a + 1]
                )
            return sum_sq

        def inverse_rms(sum_sq):
            inv_rms = work.tile([P, PAIR], F32)
            nc.scalar.activation(
                out=inv_rms[:], in_=sum_sq[:], func=ACT.Abs_reciprocal_sqrt, scale=1.0 / QL, bias=eps[:]
            )
            return inv_rms

        def normalise(banks, inv_rms):
            cn = work.tile([P, PAIR * QL], BF16)
            for a in range(PAIR):
                nc.vector.scalar_tensor_tensor(
                    out=cn[:, a * QL : (a + 1) * QL],
                    in0=banks[a][:],
                    scalar=inv_rms[:, a : a + 1],
                    in1=gain[:],
                    op0=ALU.mult,
                    op1=ALU.mult,
                )
            return cn

        def rope_products(q_bank, vecs):
            n = vecs.stop - vecs.start
            q = q_bank[:].rearrange("p a (h d) -> p (a h) d", d=HEAD)
            products = work.tile([P, VECS, 2, ROT], F32)
            nc.vector.tensor_tensor(
                out=products[:, vecs],
                in0=q[:, vecs, ROT:HEAD].unsqueeze(2).to_broadcast([P, n, 2, ROT]),
                in1=trig[:, vecs],
                op=ALU.mult,
            )
            return products

        def plain_values(q_bank, vecs, copy):
            q = q_bank[:].rearrange("p a (h d) -> p (a h) d", d=HEAD)
            result = work.tile([P, VECS, HEAD], F32)
            copy(out=result[:, vecs, 0:ROT], in_=q[:, vecs, 0:ROT])
            return result

        def rope_sum(products, result, g, vecs):
            by_half = products[:, vecs].rearrange("p v x (s j) -> p v x s j", s=2)
            nc.vector.tensor_tensor(
                out=result[:, vecs, ROT:HEAD].rearrange("p v (s j) -> p v s j", s=2),
                in0=by_half[:, :, 0],
                in1=by_half[:, :, 1, ::-1, :],
                op=ALU.add,
            )
            nc.sync.dma_start(
                out=out_groups[g][:, vecs.start * HEAD : vecs.stop * HEAD],
                in_=result[:, vecs].rearrange("p v d -> p (v d)"),
            )

        def live(i):
            return 0 <= i < N_PAIRS

        x_bank_of, c_banks_of, inv_rms_of, cn_of, cn_bank_of = {}, {}, {}, {}, {}
        q_bank_of, products_of, sum_sq_of = {}, {}, {}
        all_vecs = slice(0, VECS)
        both = slice(0, PAIR)

        def second_matmul(i, q_bank, tiles):
            h = i % PAIRS_IN_GROUP
            for a in range(tiles.start, tiles.stop):
                multiply(q_bank[:, h * PAIR + a, :], mx_of[i + 1], PAIR + a, wb_codes, wb_scales)

        def one_round(i, vector_copies_x):
            if live(i + 1):
                sum_sq_of[i + 1] = square_sums(c_banks_of[i + 1])
                if vector_copies_x:
                    inv_rms_of[i + 1] = inverse_rms(sum_sq_of[i + 1])
            if live(i):
                cn_of[i] = normalise(c_banks_of[i], inv_rms_of[i])
                cn_bank_of[i] = transpose_pair(cn_words(cn_of[i]), "cn", warm=True)
            g, second = divmod(i - ROPE_LAG, PAIRS_IN_GROUP)
            if g >= 0 and second == 0:
                products_of[g] = rope_products(q_bank_of[g], all_vecs)
            if g >= 0 and second == 1:
                result = plain_values(q_bank_of[g], all_vecs, nc.vector.tensor_copy)
                rope_sum(products_of[g], result, g, all_vecs)
            if live(i + 2):
                c_banks_of[i + 2] = first_matmul(i + 2)
            with_x, with_cn = live(i + X_LEAD), live(i - 1)
            quantise(i, X if with_x else PAIR, PAIR * (with_x + with_cn))
            if with_cn:
                g, h = divmod(i - 1, PAIRS_IN_GROUP)
                if h == 0:
                    q_bank = psum_q.tile([P, GROUP, OUT], F32)
                    q_bank_of[g] = q_bank
                second_matmul(i - 1, q_bank_of[g], both)
            if live(i + 1 + X_LEAD):
                copy = nc.vector.tensor_copy if vector_copies_x else nc.scalar.copy
                regroup(x_bank_of[i + 1 + X_LEAD], i + 1, X, both, copy)
            if live(i + 1) and not vector_copies_x:
                inv_rms_of[i + 1] = inverse_rms(sum_sq_of[i + 1])
            if live(i + 2 + X_LEAD):
                x_bank_of[i + 2 + X_LEAD] = transpose_pair(x_words(x_tiles[i + 2 + X_LEAD]), "x")
            if live(i):
                regroup(cn_bank_of[i], i + 1, CN, both, nc.scalar.copy)

        x_bank_of[0] = transpose_pair(x_words(x_tiles[0]), "x")
        regroup(x_bank_of[0], -X_LEAD, X, both, nc.vector.tensor_copy)
        x_bank_of[1] = transpose_pair(x_words(x_tiles[1]), "x")
        regroup_wa(nc.scalar.copy, wa_raw, wa_grouped, 1, slice(P // 2, P))
        regroup_wa(nc.vector.tensor_copy, wa_raw, wa_grouped, 0, slice(0, P))
        regroup_wa(nc.vector.tensor_copy, wa_raw, wa_grouped, 1, slice(0, P // 2))
        quantise(-X_LEAD, X, PAIR)
        wa_codes, wa_scales = quantise_weight(nc, const, wa_grouped, QL, "wa")
        gain_bank = psum_q.tile([P, GROUP, OUT], F32, name="q_bank")
        nc.tensor.matmul(
            gain_bank[:].rearrange("p a o -> p (a o)"), lhsT=ones[:], rhs=gain_row[:], start=True, stop=True
        )
        regroup(x_bank_of[1], 1 - X_LEAD, X, both, nc.scalar.copy)
        x_bank_of[2] = transpose_pair(x_words(x_tiles[2]), "x")
        one_round(-2, True)
        wb_codes, wb_scales = quantise_weight(nc, const, wb_grouped, OUT, "wb")
        gain = const.tile([P, QL], BF16)
        nc.scalar.copy(
            out=gain[:].rearrange("p (u m e) -> p u m e", u=2, e=2),
            in_=gain_bank[:].rearrange("p a o -> p (a o)").rearrange("p (m u e) -> p u m e", u=2, e=2),
        )
        for i in range(-1, N_PAIRS - 1):
            one_round(i, i < ROPE_LAG)

        last = N_PAIRS - 1
        g = N_GROUPS - 1
        halves = [slice(0, VECS // 2), slice(VECS // 2, VECS)]
        cn_of[last] = normalise(c_banks_of[last], inv_rms_of[last])
        cn_bank_of[last] = transpose_pair(cn_words(cn_of[last]), "cn")
        result = plain_values(q_bank_of[g - 1], all_vecs, nc.scalar.copy)
        products_of[g - 1] = rope_products(q_bank_of[g - 1], all_vecs)
        q_banks = []
        for half in halves:
            q_bank = psum_q.tile([P, GROUP, OUT], F32)
            q_banks.append(q_bank)
        quantise(last, PAIR, PAIR)
        second_matmul(last - 1, q_banks[0], both)
        for a in range(PAIR):
            tile = slice(a, a + 1)
            regroup(cn_bank_of[last], N_PAIRS, CN, tile, nc.scalar.copy)
            quantise(N_PAIRS, PAIR + a, 1)
            second_matmul(last, q_banks[1], tile)
        rope_sum(products_of[g - 1], result, g - 1, all_vecs)
        first_result = plain_values(q_banks[0], halves[0], nc.scalar.copy)
        first_products = rope_products(q_banks[0], halves[0])
        second_products = rope_products(q_banks[1], halves[1])
        second_result = plain_values(q_banks[1], halves[1], nc.scalar.copy)
        rope_sum(first_products, first_result, g, halves[0])
        rope_sum(second_products, second_result, g, halves[1])
